import numpy as np
import ml_dtypes


def mxq(x, axis, fmt="e4m3"):
    dtype, down = {"e4m3": (ml_dtypes.float8_e4m3fn, 7), "e5m2": (ml_dtypes.float8_e5m2, 14)}[fmt]
    v = np.moveaxis(np.asarray(x, np.float32).astype(ml_dtypes.bfloat16).astype(np.float64), axis, -1)
    blocks = v.reshape(v.shape[:-1] + (-1, 32))
    amax = np.abs(blocks).max(-1, keepdims=True)
    byte = np.maximum(np.where(amax > 0, np.frexp(amax)[1] - 1 + 127, 0) - down, 1)
    scale = np.exp2(byte - 127.0)
    codes = (blocks / scale).astype(np.float32).astype(dtype).astype(np.float64)
    return np.moveaxis((codes * scale).reshape(v.shape), -1, axis)


WIDE = False


def mx_kscale(k):
    if not WIDE:
        return np.ones(k)
    levels = np.array([10, -10, 5, -5, 0])
    a = np.random.permutation(np.resize(levels, k // 512 * 4)).reshape(k // 512, 4)
    idx = np.arange(k)
    return np.exp2(a[idx // 512, idx % 128 // 32])


BF16 = ml_dtypes.bfloat16


def bf(x):
    return np.asarray(x, np.float32).astype(BF16)


def f64(x):
    return np.asarray(x).astype(np.float64)


T, B, I, H = 128, 128, 512, 128


def sigmoid(v):
    return 1.0 / (1.0 + np.exp(-v))


def setup_inputs():
    s = mx_kscale(I)
    return {
        "input": bf(np.random.standard_normal((T, B, I)) * s),
        "h0": bf(np.random.standard_normal((B, H))),
        "c0": bf(np.random.standard_normal((B, H))),
        "noise": bf(np.random.standard_normal((B, H)) * 0.3),
        "W_ih": bf(np.random.standard_normal((4 * H, I)) / np.sqrt(I) / s[None, :]),
        "W_hh": bf(np.random.standard_normal((4 * H, H)) * 0.7 / np.sqrt(H)),
        "b_ih": bf(np.random.standard_normal(4 * H) * 0.3),
        "b_hh": bf(np.random.standard_normal(4 * H) * 0.3),
    }


def reference(input, h0, c0, noise, W_ih, W_hh, b_ih, b_hh):
    hsz = h0.shape[-1]
    gx = mxq(f64(input), 2, "e4m3") @ mxq(f64(W_ih), 1, "e4m3").T
    gh = f64(h0) @ f64(W_hh).T
    gates = gx + gh[None, :, :] + (f64(b_ih) + f64(b_hh))
    i_g = sigmoid(gates[..., 0 * hsz:1 * hsz])
    f_g = sigmoid(gates[..., 1 * hsz:2 * hsz])
    g_g = np.tanh(gates[..., 2 * hsz:3 * hsz])
    o_g = sigmoid(gates[..., 3 * hsz:4 * hsz])
    c = f_g * f64(c0)[None] + i_g * g_g
    h = o_g * np.tanh(c) + f64(noise)[None]
    return (h, np.stack([h[-1], c[-1]]))

@@ -1,0 +1,244 @@
+from contextlib import ExitStack
+
+import concourse.mybir as mybir
+from concourse.masks import make_identity
+
+F32 = mybir.dt.float32
+BF16 = mybir.dt.bfloat16
+U32 = mybir.dt.uint32
+U8 = mybir.dt.uint8
+FP8X4 = mybir.dt.float8_e4m3fn_x4
+AF = mybir.ActivationFunctionType
+ALU = mybir.AluOpType
+
+T, B, I, H = 128, 128, 512, 128
+P = 128
+GB = 4
+NG = B // GB
+COLS = GB * T
+FLOPS = 2 * T * B * I * 4 * H + 2 * B * H * 4 * H
+
+LEAD = 7
+XBUFS = 8
+MANUAL = True
+R_POOL_EVERY = 0
+GATE_ORDER = (0, 2, 1, 3)
+NCH = 8
+GPC = NG // NCH
+
+
+def tile_lstmlayer_t_kernel(tc, x, h0, c0, noise, w_ih, w_hh, b_ih, b_hh, out_0, out_1):
+    nc = tc.nc
+    with ExitStack() as ctx:
+        const = ctx.enter_context(tc.tile_pool(name="const", bufs=1))
+        xpool = ctx.enter_context(tc.tile_pool(name="xin", bufs=XBUFS))
+        work = ctx.enter_context(tc.tile_pool(name="work", bufs=3))
+        ps1 = ctx.enter_context(tc.psum_pool(name="ps1", bufs=1))
+        ps2 = ctx.enter_context(tc.psum_pool(name="ps2", bufs=2))
+        if MANUAL:
+            ctx.enter_context(tc.manual_schedule())
+
+        tl = {}
+
+        def load(g):
+            t = xpool.tile([P, GB * I], BF16, name="x%d" % g, tag="x")
+            nc.sync.dma_start(out=t[:], in_=x[:, GB * g:GB * (g + 1), :].rearrange("t b k -> t (b k)"))
+            tl[("x", g)] = t
+
+        def load_noise(c):
+            t = const.tile([P, GPC * COLS], BF16, name="nz%d" % c, tag="nz%d" % c)
+            src = noise[GPC * GB * c:GPC * GB * (c + 1), :].rearrange("b u -> (b u)")
+            nc.sync.dma_start(out=t[:], in_=src.partition_broadcast(P))
+            tl[("nz", c)] = t
+
+        def transposes_in(src_f32, key):
+            grp = work.tile([P, 4 * COLS], BF16, name="grp_%s" % key, tag="grp", align_bytes=64)
+            gv = grp[:].bitcast(F32).rearrange("p (b r u) -> p b r u", b=4, u=2)
+            halves = []
+            for hf in range(2):
+                xt = ps2.tile([P, 2, 2, P], F32, name="xt_%s_%d" % (key, hf), tag="xt")
+                for bb in range(2):
+                    for u in range(2):
+                        c0_ = (2 * hf + bb) * 256 + u * P
+                        nc.tensor.transpose(xt[:, bb, u, :], src_f32[:, c0_:c0_ + P], ident_f[:])
+                halves.append(xt)
+            return grp, gv, halves
+
+        def t_in(g):
+            xs = tl.pop(("x", g))
+            tl[("grp", g)] = transposes_in(xs[:].bitcast(F32), "g%d" % g)
+
+        def evac_in(g):
+            grp, gv, halves = tl[("grp", g)]
+            for hf in range(2):
+                nc.vector.tensor_copy(out=gv[:, 2 * hf:2 * hf + 2], in_=halves[hf][:].rearrange("p b u r -> p b r u"))
+
+        def quant(g):
+            grp, gv, halves = tl.pop(("grp", g))
+            codes = work.tile([P, COLS], U32, name="codes%d" % g, tag="codes", align_bytes=64)
+            scl = work.tile([P, COLS], U8, name="scl%d" % g, tag="scl", align_bytes=64)
+            nc.vector.quantize_mx(out=codes[:].bitcast(FP8X4), scales=scl[:], in_=grp[:])
+            tl[("q", g)] = (codes, scl)
+
+        def mx(g):
+            codes, scl = tl.pop(("q", g))
+            for j in GATE_ORDER:
+                gp = ps1.tile([P, COLS], F32, name="gp%d_%d" % (j, g), tag="gp%d" % j)
+                nc.tensor.matmul_mx(
+                    out=gp[:],
+                    lhsT=w_codes[:, j * P:(j + 1) * P].bitcast(FP8X4),
+                    lhsT_scale=w_scl[:, j * P:(j + 1) * P],
+                    rhs=codes[:].bitcast(FP8X4),
+                    rhs_scale=scl[:],
+                    start=True,
+                    stop=True,
+                )
+                tl[("gp", j, g)] = gp
+
+        def acts(g):
+            for j in GATE_ORDER:
+                gp = tl.pop(("gp", j, g))
+                gs = work.tile([P, COLS], F32, name="gs%d_%d" % (j, g), tag="gs%d" % j)
+                fn = AF.Tanh if j == 2 else AF.Sigmoid
+                for b in range(GB):
+                    col = j * B + GB * g + b
+                    nc.scalar.activation(out=gs[:, b * T:(b + 1) * T], in_=gp[:, b * T:(b + 1) * T], func=fn,
+                                         bias=gt[:, col:col + 1], scale=1.0)
+                tl[("gs", j, g)] = gs
+                if j == 2:
+                    pt = work.tile([P, COLS], F32, name="pt%d" % g, tag="pt")
+                    nc.gpsimd.tensor_tensor(out=pt[:], in0=tl.pop(("gs", 0, g))[:], in1=tl.pop(("gs", 2, g))[:], op=ALU.mult)
+                    tl[("pt", g)] = pt
+
+        def cell(g):
+            pt = tl.pop(("pt", g))
+            f = tl.pop(("gs", 1, g))
+            c = work.tile([P, COLS], F32, name="c%d" % g, tag="c")
+            for b in range(GB):
+                nc.vector.scalar_tensor_tensor(out=c[:, b * T:(b + 1) * T], in0=f[:, b * T:(b + 1) * T],
+                                               scalar=c0t[:, GB * g + b:GB * g + b + 1], in1=pt[:, b * T:(b + 1) * T],
+                                               op0=ALU.mult, op1=ALU.add)
+            nc.gpsimd.tensor_copy(out=cl[:, GB * g:GB * (g + 1)], in_=c[:].rearrange("p (b t) -> p b t", t=T)[:, :, T - 1])
+            tl[("c", g)] = c
+
+        def tanh_c(g):
+            c = tl.pop(("c", g))
+            tcn = work.tile([P, COLS], F32, name="tc%d" % g, tag="tc")
+            nc.scalar.activation(out=tcn[:], in_=c[:], func=AF.Tanh)
+            tl[("tc", g)] = tcn
+
+        def r_mul(g):
+            tcn = tl.pop(("tc", g))
+            o = tl.pop(("gs", 3, g))
+            r = work.tile([P, COLS], F32, name="r%d" % g, tag="r")
+            eng = nc.gpsimd if (R_POOL_EVERY and g % R_POOL_EVERY == 0) else nc.vector
+            eng.tensor_tensor(out=r[:], in0=o[:], in1=tcn[:], op=ALU.mult)
+            tl[("r", g)] = r
+
+        def t_out(g):
+            r = tl.pop(("r", g))
+            ht = ps2.tile([P, COLS], F32, name="ht%d" % g, tag="ht")
+            for b in range(GB):
+                nc.tensor.transpose(ht[:, b * H:(b + 1) * H], r[:, b * T:(b + 1) * T], ident_f[:])
+            tl[("ht", g)] = ht
+
+        def h_out(g):
+            ht = tl.pop(("ht", g))
+            hs = work.tile([P, COLS], F32, name="hs%d" % g, tag="hs")
+            nz = tl[("nz", g // GPC)]
+            k = g % GPC
+            nc.vector.tensor_tensor(out=hs[:], in0=ht[:], in1=nz[:, k * COLS:(k + 1) * COLS], op=ALU.add)
+            nc.sync.dma_start(out=out_0[:, GB * g:GB * (g + 1), :].rearrange("t b u -> t (b u)"), in_=hs[:])
+            nc.sync.dma_start(out=out_1[0:1, GB * g:GB * (g + 1), :].rearrange("o b u -> o (b u)"), in_=hs[T - 1:T, :])
+
+        w_sb = const.tile([P, 4 * I], BF16, name="w_sb", tag="w_sb")
+        nc.sync.dma_start(out=w_sb[:].rearrange("p (j k) -> p j k", j=4), in_=w_ih.rearrange("(j p) k -> p j k", p=P))
+        load(0)
+        whh_sb = const.tile([P, 4 * H], BF16, name="whh_sb", tag="whh_sb")
+        nc.scalar.dma_start(out=whh_sb[:].rearrange("p (j k) -> p j k", j=4), in_=w_hh.rearrange("(j p) k -> p j k", p=P))
+        h0_sb = const.tile([P, H], BF16, name="h0_sb", tag="h0_sb")
+        nc.scalar.dma_start(out=h0_sb[:], in_=h0)
+        c0_sb = const.tile([P, H], BF16, name="c0_sb", tag="c0_sb")
+        nc.scalar.dma_start(out=c0_sb[:], in_=c0)
+        bz = const.tile([P, 4 * H], BF16, name="bz", tag="bz")
+        nc.vector.memset(bz[:], 0.0)
+        ones = const.tile([P, B], BF16, name="ones", tag="ones")
+        nc.vector.memset(ones[:], 1.0)
+        nc.scalar.dma_start(out=bz[0:1, :], in_=b_ih.rearrange("(o n) -> o n", o=1))
+        nc.scalar.dma_start(out=bz[1:2, :], in_=b_hh.rearrange("(o n) -> o n", o=1))
+        ident_f = const.tile([P, P], F32, name="ident_f", tag="ident_f")
+        make_identity(nc, ident_f[:])
+        ident_b = const.tile([P, P], BF16, name="ident_b", tag="ident_b")
+        make_identity(nc, ident_b[:])
+        for g in range(1, 3):
+            load(g)
+        load_noise(0)
+        for g in range(3, LEAD):
+            load(g)
+        load_noise(1)
+
+        cl = const.tile([P, B], F32, name="cl", tag="cl")
+
+        w_grp, w_gv, w_halves = transposes_in(w_sb[:].bitcast(F32), "w")
+        nc.vector.tensor_copy(out=w_gv[:, 0:2], in_=w_halves[0][:].rearrange("p b u r -> p b r u"))
+        nc.scalar.copy(out=w_gv[:, 2:4], in_=w_halves[1][:].rearrange("p b u r -> p b r u"))
+        w_codes = const.tile([P, 4 * H], U32, name="w_codes", tag="w_codes", align_bytes=64)
+        w_scl = const.tile([P, 4 * H], U8, name="w_scl", tag="w_scl", align_bytes=64)
+        t_in(0)
+        evac_in(0)
+        nc.vector.quantize_mx(out=w_codes[:].bitcast(FP8X4), scales=w_scl[:], in_=w_grp[:])
+
+        sm_ps = ps2.tile([P, 6, P], BF16, name="sm_ps", tag="ht")
+        for j in range(4):
+            nc.tensor.transpose(sm_ps[:, j, :], whh_sb[:, j * H:(j + 1) * H], ident_b[:])
+        nc.tensor.transpose(sm_ps[:, 4, :], h0_sb[:], ident_b[:])
+        nc.tensor.transpose(sm_ps[:, 5, :], c0_sb[:], ident_b[:])
+        sm_t = const.tile([P, 5, P], BF16, name="sm_t", tag="sm_t")
+        nc.scalar.copy(out=sm_t[:], in_=sm_ps[:, 0:5, :])
+        c0t = const.tile([P, B], F32, name="c0t", tag="c0t")
+        nc.scalar.copy(out=c0t[:], in_=sm_ps[:, 5, :])
+        g_ps = ps2.tile([P, 4 * B], F32, name="g_ps", tag="ht")
+        for j in range(4):
+            nc.tensor.matmul(g_ps[:, j * B:(j + 1) * B], lhsT=sm_t[:, j, :], rhs=sm_t[:, 4, :], start=True, stop=False)
+            nc.tensor.matmul(g_ps[:, j * B:(j + 1) * B], lhsT=bz[:, j * H:(j + 1) * H], rhs=ones[:], start=False, stop=True)
+        gt = const.tile([P, 4 * B], F32, name="gt", tag="gt")
+        nc.scalar.copy(out=gt[:], in_=g_ps[:])
+
+        t_in(1)
+        evac_in(1)
+        quant(0)
+        t_in(2)
+        evac_in(2)
+        quant(1)
+        mx(0)
+
+        for it in range(NG + 3):
+            if it + LEAD < NG:
+                load(it + LEAD)
+            if it % GPC == 0 and it // GPC + 2 < NCH:
+                load_noise(it // GPC + 2)
+            if 0 <= it - 1 < NG:
+                cell(it - 1)
+            if it + 3 < NG:
+                t_in(it + 3)
+            if 0 <= it - 2 < NG:
+                r_mul(it - 2)
+                t_out(it - 2)
+            if it + 1 < NG:
+                mx(it + 1)
+            if it < NG:
+                acts(it)
+            if 0 <= it - 1 < NG:
+                tanh_c(it - 1)
+            if it + 3 < NG:
+                evac_in(it + 3)
+            if 0 <= it - 2 < NG:
+                h_out(it - 2)
+            if it + 2 < NG:
+                quant(it + 2)
+
+        cl_ps = ps2.tile([P, H], F32, name="cl_ps", tag="xt")
+        nc.tensor.transpose(cl_ps[:], cl[:], ident_f[:])
+        cl_sb = const.tile([P, H], F32, name="cl_sb", tag="cl_sb")
+        nc.vector.tensor_copy(out=cl_sb[:], in_=cl_ps[:])
+        nc.sync.dma_start(out=out_1[1], in_=cl_sb[:])

@@ -21,7 +21,7 @@ FLOPS = 2 * T * B * I * 4 * H + 2 * B * H * 4 * H
 LEAD = 7
 XBUFS = 8
 MANUAL = True
-R_POOL_EVERY = 0
+R_POOL_EVERY = 1
 GATE_ORDER = (0, 2, 1, 3)
 NCH = 8
 GPC = NG // NCH

@@ -25,6 +25,7 @@ R_POOL_EVERY = 1
 GATE_ORDER = (0, 2, 1, 3)
 NCH = 8
 GPC = NG // NCH
+E_ACT_EVERY = 0
 
 
 def tile_lstmlayer_t_kernel(tc, x, h0, c0, noise, w_ih, w_hh, b_ih, b_hh, out_0, out_1):
@@ -51,12 +52,12 @@ def tile_lstmlayer_t_kernel(tc, x, h0, c0, noise, w_ih, w_hh, b_ih, b_hh, out_0,
             nc.sync.dma_start(out=t[:], in_=src.partition_broadcast(P))
             tl[("nz", c)] = t
 
-        def transposes_in(src_f32, key):
+        def transposes_in(src_f32, key, tag="xt"):
             grp = work.tile([P, 4 * COLS], BF16, name="grp_%s" % key, tag="grp", align_bytes=64)
             gv = grp[:].bitcast(F32).rearrange("p (b r u) -> p b r u", b=4, u=2)
             halves = []
             for hf in range(2):
-                xt = ps2.tile([P, 2, 2, P], F32, name="xt_%s_%d" % (key, hf), tag="xt")
+                xt = ps2.tile([P, 2, 2, P], F32, name="xt_%s_%d" % (key, hf), tag=tag)
                 for bb in range(2):
                     for u in range(2):
                         c0_ = (2 * hf + bb) * 256 + u * P
@@ -68,10 +69,13 @@ def tile_lstmlayer_t_kernel(tc, x, h0, c0, noise, w_ih, w_hh, b_ih, b_hh, out_0,
             xs = tl.pop(("x", g))
             tl[("grp", g)] = transposes_in(xs[:].bitcast(F32), "g%d" % g)
 
-        def evac_in(g):
+        def evac_in(g, second_on_act=False):
             grp, gv, halves = tl[("grp", g)]
-            for hf in range(2):
-                nc.vector.tensor_copy(out=gv[:, 2 * hf:2 * hf + 2], in_=halves[hf][:].rearrange("p b u r -> p b r u"))
+            nc.vector.tensor_copy(out=gv[:, 0:2], in_=halves[0][:].rearrange("p b u r -> p b r u"))
+            if second_on_act or (E_ACT_EVERY and g % E_ACT_EVERY == 0):
+                nc.scalar.copy(out=gv[:, 2:4], in_=halves[1][:].rearrange("p b u r -> p b r u"))
+            else:
+                nc.vector.tensor_copy(out=gv[:, 2:4], in_=halves[1][:].rearrange("p b u r -> p b r u"))
 
         def quant(g):
             grp, gv, halves = tl.pop(("grp", g))
@@ -107,7 +111,8 @@ def tile_lstmlayer_t_kernel(tc, x, h0, c0, noise, w_ih, w_hh, b_ih, b_hh, out_0,
                 tl[("gs", j, g)] = gs
                 if j == 2:
                     pt = work.tile([P, COLS], F32, name="pt%d" % g, tag="pt")
-                    nc.gpsimd.tensor_tensor(out=pt[:], in0=tl.pop(("gs", 0, g))[:], in1=tl.pop(("gs", 2, g))[:], op=ALU.mult)
+                    peng = nc.vector if g == NG - 1 else nc.gpsimd
+                    peng.tensor_tensor(out=pt[:], in0=tl.pop(("gs", 0, g))[:], in1=tl.pop(("gs", 2, g))[:], op=ALU.mult)
                     tl[("pt", g)] = pt
 
         def cell(g):
@@ -118,8 +123,11 @@ def tile_lstmlayer_t_kernel(tc, x, h0, c0, noise, w_ih, w_hh, b_ih, b_hh, out_0,
                 nc.vector.scalar_tensor_tensor(out=c[:, b * T:(b + 1) * T], in0=f[:, b * T:(b + 1) * T],
                                                scalar=c0t[:, GB * g + b:GB * g + b + 1], in1=pt[:, b * T:(b + 1) * T],
                                                op0=ALU.mult, op1=ALU.add)
-            nc.gpsimd.tensor_copy(out=cl[:, GB * g:GB * (g + 1)], in_=c[:].rearrange("p (b t) -> p b t", t=T)[:, :, T - 1])
             tl[("c", g)] = c
+
+        def cl_copy(g):
+            c = tl[("c", g)]
+            nc.gpsimd.tensor_copy(out=cl[:, GB * g:GB * (g + 1)], in_=c[:].rearrange("p (b t) -> p b t", t=T)[:, :, T - 1])
 
         def tanh_c(g):
             c = tl.pop(("c", g))
@@ -131,7 +139,7 @@ def tile_lstmlayer_t_kernel(tc, x, h0, c0, noise, w_ih, w_hh, b_ih, b_hh, out_0,
             tcn = tl.pop(("tc", g))
             o = tl.pop(("gs", 3, g))
             r = work.tile([P, COLS], F32, name="r%d" % g, tag="r")
-            eng = nc.gpsimd if (R_POOL_EVERY and g % R_POOL_EVERY == 0) else nc.vector
+            eng = nc.gpsimd if (R_POOL_EVERY and g % R_POOL_EVERY == 0 and g < NG - 2) else nc.vector
             eng.tensor_tensor(out=r[:], in0=o[:], in1=tcn[:], op=ALU.mult)
             tl[("r", g)] = r
 
@@ -151,25 +159,34 @@ def tile_lstmlayer_t_kernel(tc, x, h0, c0, noise, w_ih, w_hh, b_ih, b_hh, out_0,
             nc.sync.dma_start(out=out_0[:, GB * g:GB * (g + 1), :].rearrange("t b u -> t (b u)"), in_=hs[:])
             nc.sync.dma_start(out=out_1[0:1, GB * g:GB * (g + 1), :].rearrange("o b u -> o (b u)"), in_=hs[T - 1:T, :])
 
+        def tail_piece(g, b, tcn, o, r, ht):
+            sl = slice(b * T, (b + 1) * T)
+            nc.scalar.activation(out=tcn[:, sl], in_=tl[("c", g)][:, sl], func=AF.Tanh)
+            nc.vector.tensor_tensor(out=r[:, sl], in0=o[:, sl], in1=tcn[:, sl], op=ALU.mult)
+            nc.tensor.transpose(ht[:, (b % 2) * H:(b % 2 + 1) * H], r[:, sl], ident_f[:])
+
+        ident_f = const.tile([P, P], F32, name="ident_f", tag="ident_f")
+        make_identity(nc, ident_f[:])
+        ident_b = const.tile([P, P], BF16, name="ident_b", tag="ident_b")
+        make_identity(nc, ident_b[:])
         w_sb = const.tile([P, 4 * I], BF16, name="w_sb", tag="w_sb")
-        nc.sync.dma_start(out=w_sb[:].rearrange("p (j k) -> p j k", j=4), in_=w_ih.rearrange("(j p) k -> p j k", p=P))
+        w_dst = w_sb[:].rearrange("p (j k) -> p j k", j=4)
+        w_src = w_ih.rearrange("(j p) k -> p j k", p=P)
+        nc.sync.dma_start(out=w_dst[:, 0:2], in_=w_src[:, 0:2])
+        nc.sync.dma_start(out=w_dst[:, 2:4], in_=w_src[:, 2:4])
         load(0)
         whh_sb = const.tile([P, 4 * H], BF16, name="whh_sb", tag="whh_sb")
         nc.scalar.dma_start(out=whh_sb[:].rearrange("p (j k) -> p j k", j=4), in_=w_hh.rearrange("(j p) k -> p j k", p=P))
         h0_sb = const.tile([P, H], BF16, name="h0_sb", tag="h0_sb")
         nc.scalar.dma_start(out=h0_sb[:], in_=h0)
-        c0_sb = const.tile([P, H], BF16, name="c0_sb", tag="c0_sb")
-        nc.scalar.dma_start(out=c0_sb[:], in_=c0)
         bz = const.tile([P, 4 * H], BF16, name="bz", tag="bz")
         nc.vector.memset(bz[:], 0.0)
         ones = const.tile([P, B], BF16, name="ones", tag="ones")
         nc.vector.memset(ones[:], 1.0)
         nc.scalar.dma_start(out=bz[0:1, :], in_=b_ih.rearrange("(o n) -> o n", o=1))
         nc.scalar.dma_start(out=bz[1:2, :], in_=b_hh.rearrange("(o n) -> o n", o=1))
-        ident_f = const.tile([P, P], F32, name="ident_f", tag="ident_f")
-        make_identity(nc, ident_f[:])
-        ident_b = const.tile([P, P], BF16, name="ident_b", tag="ident_b")
-        make_identity(nc, ident_b[:])
+        c0_sb = const.tile([P, H], BF16, name="c0_sb", tag="c0_sb")
+        nc.scalar.dma_start(out=c0_sb[:], in_=c0)
         for g in range(1, 3):
             load(g)
         load_noise(0)
@@ -179,16 +196,17 @@ def tile_lstmlayer_t_kernel(tc, x, h0, c0, noise, w_ih, w_hh, b_ih, b_hh, out_0,
 
         cl = const.tile([P, B], F32, name="cl", tag="cl")
 
-        w_grp, w_gv, w_halves = transposes_in(w_sb[:].bitcast(F32), "w")
+        w_grp, w_gv, w_halves = transposes_in(w_sb[:].bitcast(F32), "w", tag="ht")
         nc.vector.tensor_copy(out=w_gv[:, 0:2], in_=w_halves[0][:].rearrange("p b u r -> p b r u"))
         nc.scalar.copy(out=w_gv[:, 2:4], in_=w_halves[1][:].rearrange("p b u r -> p b r u"))
         w_codes = const.tile([P, 4 * H], U32, name="w_codes", tag="w_codes", align_bytes=64)
         w_scl = const.tile([P, 4 * H], U8, name="w_scl", tag="w_scl", align_bytes=64)
         t_in(0)
-        evac_in(0)
+        evac_in(0, second_on_act=True)
         nc.vector.quantize_mx(out=w_codes[:].bitcast(FP8X4), scales=w_scl[:], in_=w_grp[:])
+        quant(0)
 
-        sm_ps = ps2.tile([P, 6, P], BF16, name="sm_ps", tag="ht")
+        sm_ps = ps1.tile([P, 6, P], BF16, name="sm_ps", tag="gp3")
         for j in range(4):
             nc.tensor.transpose(sm_ps[:, j, :], whh_sb[:, j * H:(j + 1) * H], ident_b[:])
         nc.tensor.transpose(sm_ps[:, 4, :], h0_sb[:], ident_b[:])
@@ -196,28 +214,26 @@ def tile_lstmlayer_t_kernel(tc, x, h0, c0, noise, w_ih, w_hh, b_ih, b_hh, out_0,
         sm_t = const.tile([P, 5, P], BF16, name="sm_t", tag="sm_t")
         nc.scalar.copy(out=sm_t[:], in_=sm_ps[:, 0:5, :])
         c0t = const.tile([P, B], F32, name="c0t", tag="c0t")
-        nc.scalar.copy(out=c0t[:], in_=sm_ps[:, 5, :])
-        g_ps = ps2.tile([P, 4 * B], F32, name="g_ps", tag="ht")
+        t_in(1)
+        g_ps = ps1.tile([P, 4 * B], F32, name="g_ps", tag="gp1")
         for j in range(4):
             nc.tensor.matmul(g_ps[:, j * B:(j + 1) * B], lhsT=sm_t[:, j, :], rhs=sm_t[:, 4, :], start=True, stop=False)
             nc.tensor.matmul(g_ps[:, j * B:(j + 1) * B], lhsT=bz[:, j * H:(j + 1) * H], rhs=ones[:], start=False, stop=True)
         gt = const.tile([P, 4 * B], F32, name="gt", tag="gt")
         nc.scalar.copy(out=gt[:], in_=g_ps[:])
-
-        t_in(1)
+        nc.scalar.copy(out=c0t[:], in_=sm_ps[:, 5, :])
+        mx(0)
         evac_in(1)
-        quant(0)
+        quant(1)
         t_in(2)
         evac_in(2)
-        quant(1)
-        mx(0)
 
-        for it in range(NG + 3):
+        for it in range(NG):
             if it + LEAD < NG:
                 load(it + LEAD)
             if it % GPC == 0 and it // GPC + 2 < NCH:
                 load_noise(it // GPC + 2)
-            if 0 <= it - 1 < NG:
+            if 0 <= it - 1 < NG - 1:
                 cell(it - 1)
             if it + 3 < NG:
                 t_in(it + 3)
@@ -228,7 +244,12 @@ def tile_lstmlayer_t_kernel(tc, x, h0, c0, noise, w_ih, w_hh, b_ih, b_hh, out_0,
                 mx(it + 1)
             if it < NG:
                 acts(it)
-            if 0 <= it - 1 < NG:
+            if 0 <= it - 1 < NG - 1:
+                cl_copy(it - 1)
+            if it == NG - 1:
+                cell(it)
+                cl_copy(it)
+            if 0 <= it - 1 < NG - 1:
                 tanh_c(it - 1)
             if it + 3 < NG:
                 evac_in(it + 3)
@@ -237,8 +258,26 @@ def tile_lstmlayer_t_kernel(tc, x, h0, c0, noise, w_ih, w_hh, b_ih, b_hh, out_0,
             if it + 2 < NG:
                 quant(it + 2)
 
+        r_mul(NG - 2)
+        t_out(NG - 2)
+        g = NG - 1
         cl_ps = ps2.tile([P, H], F32, name="cl_ps", tag="xt")
         nc.tensor.transpose(cl_ps[:], cl[:], ident_f[:])
+        tcn = work.tile([P, COLS], F32, name="tc_last", tag="tc")
+        r = work.tile([P, COLS], F32, name="r_last", tag="r")
+        o = tl.pop(("gs", 3, g))
+        ht_halves = [ps1.tile([P, 2 * H], F32, name="ht_last0", tag="gp0"), ps1.tile([P, 2 * H], F32, name="ht_last1", tag="gp2")]
+        hs = work.tile([P, COLS], F32, name="hs_last", tag="hs")
+        nz = tl[("nz", g // GPC)]
+        k = g % GPC
+        for b in range(GB):
+            tail_piece(g, b, tcn, o, r, ht_halves[b // 2])
+        h_out(NG - 2)
         cl_sb = const.tile([P, H], F32, name="cl_sb", tag="cl_sb")
         nc.vector.tensor_copy(out=cl_sb[:], in_=cl_ps[:])
         nc.sync.dma_start(out=out_1[1], in_=cl_sb[:])
+        for hf in range(2):
+            sl = slice(hf * 2 * T, (hf + 1) * 2 * T)
+            nc.vector.tensor_tensor(out=hs[:, sl], in0=ht_halves[hf][:], in1=nz[:, k * COLS + hf * 2 * T:k * COLS + (hf + 1) * 2 * T], op=ALU.add)
+            nc.sync.dma_start(out=out_0[:, GB * g + 2 * hf:GB * g + 2 * hf + 2, :].rearrange("t b u -> t (b u)"), in_=hs[:, sl])
+        nc.sync.dma_start(out=out_1[0:1, GB * g:GB * (g + 1), :].rearrange("o b u -> o (b u)"), in_=hs[T - 1:T, :])

@@ -21,11 +21,11 @@ FLOPS = 2 * T * B * I * 4 * H + 2 * B * H * 4 * H
 LEAD = 7
 XBUFS = 8
 MANUAL = True
-R_POOL_EVERY = 1
+R_POOL_EVERY = 0
 GATE_ORDER = (0, 2, 1, 3)
 NCH = 8
 GPC = NG // NCH
-E_ACT_EVERY = 0
+E_ACT_EVERY = 2
 
 
 def tile_lstmlayer_t_kernel(tc, x, h0, c0, noise, w_ih, w_hh, b_ih, b_hh, out_0, out_1):
@@ -69,10 +69,12 @@ def tile_lstmlayer_t_kernel(tc, x, h0, c0, noise, w_ih, w_hh, b_ih, b_hh, out_0,
             xs = tl.pop(("x", g))
             tl[("grp", g)] = transposes_in(xs[:].bitcast(F32), "g%d" % g)
 
-        def evac_in(g, second_on_act=False):
+        def evac_in(g, second_on_act=None):
             grp, gv, halves = tl[("grp", g)]
             nc.vector.tensor_copy(out=gv[:, 0:2], in_=halves[0][:].rearrange("p b u r -> p b r u"))
-            if second_on_act or (E_ACT_EVERY and g % E_ACT_EVERY == 0):
+            if second_on_act is None:
+                second_on_act = bool(E_ACT_EVERY) and g % E_ACT_EVERY == 0
+            if second_on_act:
                 nc.scalar.copy(out=gv[:, 2:4], in_=halves[1][:].rearrange("p b u r -> p b r u"))
             else:
                 nc.vector.tensor_copy(out=gv[:, 2:4], in_=halves[1][:].rearrange("p b u r -> p b r u"))
@@ -99,8 +101,8 @@ def tile_lstmlayer_t_kernel(tc, x, h0, c0, noise, w_ih, w_hh, b_ih, b_hh, out_0,
                 )
                 tl[("gp", j, g)] = gp
 
-        def acts(g):
-            for j in GATE_ORDER:
+        def acts(g, gates):
+            for j in gates:
                 gp = tl.pop(("gp", j, g))
                 gs = work.tile([P, COLS], F32, name="gs%d_%d" % (j, g), tag="gs%d" % j)
                 fn = AF.Tanh if j == 2 else AF.Sigmoid
@@ -223,43 +225,44 @@ def tile_lstmlayer_t_kernel(tc, x, h0, c0, noise, w_ih, w_hh, b_ih, b_hh, out_0,
         nc.scalar.copy(out=gt[:], in_=g_ps[:])
         nc.scalar.copy(out=c0t[:], in_=sm_ps[:, 5, :])
         mx(0)
-        evac_in(1)
+        evac_in(1, second_on_act=False)
         quant(1)
         t_in(2)
-        evac_in(2)
+        evac_in(2, second_on_act=False)
 
         for it in range(NG):
             if it + LEAD < NG:
                 load(it + LEAD)
             if it % GPC == 0 and it // GPC + 2 < NCH:
                 load_noise(it // GPC + 2)
-            if 0 <= it - 1 < NG - 1:
+            if 0 <= it - 1:
                 cell(it - 1)
             if it + 3 < NG:
                 t_in(it + 3)
-            if 0 <= it - 2 < NG:
+            if 0 <= it - 2:
                 r_mul(it - 2)
                 t_out(it - 2)
             if it + 1 < NG:
                 mx(it + 1)
-            if it < NG:
-                acts(it)
-            if 0 <= it - 1 < NG - 1:
+            acts(it, GATE_ORDER[0:2])
+            if 0 <= it - 3:
+                h_out(it - 3)
+            if it + 3 < NG:
+                evac_in(it + 3)
+            acts(it, GATE_ORDER[2:4])
+            if 0 <= it - 1:
                 cl_copy(it - 1)
             if it == NG - 1:
                 cell(it)
                 cl_copy(it)
-            if 0 <= it - 1 < NG - 1:
+            if 0 <= it - 1:
                 tanh_c(it - 1)
-            if it + 3 < NG:
-                evac_in(it + 3)
-            if 0 <= it - 2 < NG:
-                h_out(it - 2)
             if it + 2 < NG:
                 quant(it + 2)
 
         r_mul(NG - 2)
         t_out(NG - 2)
+        h_out(NG - 3)
         g = NG - 1
         cl_ps = ps2.tile([P, H], F32, name="cl_ps", tag="xt")
         nc.tensor.transpose(cl_ps[:], cl[:], ident_f[:])

@@ -20,7 +20,7 @@ FLOPS = 2 * T * B * I * 4 * H + 2 * B * H * 4 * H
 
 LEAD = 7
 XBUFS = 8
-MANUAL = True
+MANUAL = False
 R_POOL_EVERY = 0
 GATE_ORDER = (0, 2, 1, 3)
 NCH = 8

from contextlib import ExitStack

import concourse.mybir as mybir
from concourse.masks import make_identity

F32 = mybir.dt.float32
BF16 = mybir.dt.bfloat16
U32 = mybir.dt.uint32
U8 = mybir.dt.uint8
FP8X4 = mybir.dt.float8_e4m3fn_x4
AF = mybir.ActivationFunctionType
ALU = mybir.AluOpType

T, B, I, H = 128, 128, 512, 128
P = 128
GB = 4
NG = B // GB
COLS = GB * T
FLOPS = 2 * T * B * I * 4 * H + 2 * B * H * 4 * H

LEAD = 7
XBUFS = 8
MANUAL = False
R_POOL_EVERY = 0
GATE_ORDER = (0, 2, 1, 3)
NCH = 8
GPC = NG // NCH
E_ACT_EVERY = 2


def tile_lstmlayer_t_kernel(tc, x, h0, c0, noise, w_ih, w_hh, b_ih, b_hh, out_0, out_1):
    nc = tc.nc
    with ExitStack() as ctx:
        const = ctx.enter_context(tc.tile_pool(name="const", bufs=1))
        xpool = ctx.enter_context(tc.tile_pool(name="xin", bufs=XBUFS))
        work = ctx.enter_context(tc.tile_pool(name="work", bufs=3))
        ps1 = ctx.enter_context(tc.psum_pool(name="ps1", bufs=1))
        ps2 = ctx.enter_context(tc.psum_pool(name="ps2", bufs=2))
        if MANUAL:
            ctx.enter_context(tc.manual_schedule())

        tl = {}

        def load(g):
            t = xpool.tile([P, GB * I], BF16, name="x%d" % g, tag="x")
            nc.sync.dma_start(out=t[:], in_=x[:, GB * g:GB * (g + 1), :].rearrange("t b k -> t (b k)"))
            tl[("x", g)] = t

        def load_noise(c):
            t = const.tile([P, GPC * COLS], BF16, name="nz%d" % c, tag="nz%d" % c)
            src = noise[GPC * GB * c:GPC * GB * (c + 1), :].rearrange("b u -> (b u)")
            nc.sync.dma_start(out=t[:], in_=src.partition_broadcast(P))
            tl[("nz", c)] = t

        def transposes_in(src_f32, key, tag="xt"):
            grp = work.tile([P, 4 * COLS], BF16, name="grp_%s" % key, tag="grp", align_bytes=64)
            gv = grp[:].bitcast(F32).rearrange("p (b r u) -> p b r u", b=4, u=2)
            halves = []
            for hf in range(2):
                xt = ps2.tile([P, 2, 2, P], F32, name="xt_%s_%d" % (key, hf), tag=tag)
                for bb in range(2):
                    for u in range(2):
                        c0_ = (2 * hf + bb) * 256 + u * P
                        nc.tensor.transpose(xt[:, bb, u, :], src_f32[:, c0_:c0_ + P], ident_f[:])
                halves.append(xt)
            return grp, gv, halves

        def t_in(g):
            xs = tl.pop(("x", g))
            tl[("grp", g)] = transposes_in(xs[:].bitcast(F32), "g%d" % g)

        def evac_in(g, second_on_act=None):
            grp, gv, halves = tl[("grp", g)]
            nc.vector.tensor_copy(out=gv[:, 0:2], in_=halves[0][:].rearrange("p b u r -> p b r u"))
            if second_on_act is None:
                second_on_act = bool(E_ACT_EVERY) and g % E_ACT_EVERY == 0
            if second_on_act:
                nc.scalar.copy(out=gv[:, 2:4], in_=halves[1][:].rearrange("p b u r -> p b r u"))
            else:
                nc.vector.tensor_copy(out=gv[:, 2:4], in_=halves[1][:].rearrange("p b u r -> p b r u"))

        def quant(g):
            grp, gv, halves = tl.pop(("grp", g))
            codes = work.tile([P, COLS], U32, name="codes%d" % g, tag="codes", align_bytes=64)
            scl = work.tile([P, COLS], U8, name="scl%d" % g, tag="scl", align_bytes=64)
            nc.vector.quantize_mx(out=codes[:].bitcast(FP8X4), scales=scl[:], in_=grp[:])
            tl[("q", g)] = (codes, scl)

        def mx(g):
            codes, scl = tl.pop(("q", g))
            for j in GATE_ORDER:
                gp = ps1.tile([P, COLS], F32, name="gp%d_%d" % (j, g), tag="gp%d" % j)
                nc.tensor.matmul_mx(
                    out=gp[:],
                    lhsT=w_codes[:, j * P:(j + 1) * P].bitcast(FP8X4),
                    lhsT_scale=w_scl[:, j * P:(j + 1) * P],
                    rhs=codes[:].bitcast(FP8X4),
                    rhs_scale=scl[:],
                    start=True,
                    stop=True,
                )
                tl[("gp", j, g)] = gp

        def acts(g, gates):
            for j in gates:
                gp = tl.pop(("gp", j, g))
                gs = work.tile([P, COLS], F32, name="gs%d_%d" % (j, g), tag="gs%d" % j)
                fn = AF.Tanh if j == 2 else AF.Sigmoid
                for b in range(GB):
                    col = j * B + GB * g + b
                    nc.scalar.activation(out=gs[:, b * T:(b + 1) * T], in_=gp[:, b * T:(b + 1) * T], func=fn,
                                         bias=gt[:, col:col + 1], scale=1.0)
                tl[("gs", j, g)] = gs
                if j == 2:
                    pt = work.tile([P, COLS], F32, name="pt%d" % g, tag="pt")
                    peng = nc.vector if g == NG - 1 else nc.gpsimd
                    peng.tensor_tensor(out=pt[:], in0=tl.pop(("gs", 0, g))[:], in1=tl.pop(("gs", 2, g))[:], op=ALU.mult)
                    tl[("pt", g)] = pt

        def cell(g):
            pt = tl.pop(("pt", g))
            f = tl.pop(("gs", 1, g))
            c = work.tile([P, COLS], F32, name="c%d" % g, tag="c")
            for b in range(GB):
                nc.vector.scalar_tensor_tensor(out=c[:, b * T:(b + 1) * T], in0=f[:, b * T:(b + 1) * T],
                                               scalar=c0t[:, GB * g + b:GB * g + b + 1], in1=pt[:, b * T:(b + 1) * T],
                                               op0=ALU.mult, op1=ALU.add)
            tl[("c", g)] = c

        def cl_copy(g):
            c = tl[("c", g)]
            nc.gpsimd.tensor_copy(out=cl[:, GB * g:GB * (g + 1)], in_=c[:].rearrange("p (b t) -> p b t", t=T)[:, :, T - 1])

        def tanh_c(g):
            c = tl.pop(("c", g))
            tcn = work.tile([P, COLS], F32, name="tc%d" % g, tag="tc")
            nc.scalar.activation(out=tcn[:], in_=c[:], func=AF.Tanh)
            tl[("tc", g)] = tcn

        def r_mul(g):
            tcn = tl.pop(("tc", g))
            o = tl.pop(("gs", 3, g))
            r = work.tile([P, COLS], F32, name="r%d" % g, tag="r")
            eng = nc.gpsimd if (R_POOL_EVERY and g % R_POOL_EVERY == 0 and g < NG - 2) else nc.vector
            eng.tensor_tensor(out=r[:], in0=o[:], in1=tcn[:], op=ALU.mult)
            tl[("r", g)] = r

        def t_out(g):
            r = tl.pop(("r", g))
            ht = ps2.tile([P, COLS], F32, name="ht%d" % g, tag="ht")
            for b in range(GB):
                nc.tensor.transpose(ht[:, b * H:(b + 1) * H], r[:, b * T:(b + 1) * T], ident_f[:])
            tl[("ht", g)] = ht

        def h_out(g):
            ht = tl.pop(("ht", g))
            hs = work.tile([P, COLS], F32, name="hs%d" % g, tag="hs")
            nz = tl[("nz", g // GPC)]
            k = g % GPC
            nc.vector.tensor_tensor(out=hs[:], in0=ht[:], in1=nz[:, k * COLS:(k + 1) * COLS], op=ALU.add)
            nc.sync.dma_start(out=out_0[:, GB * g:GB * (g + 1), :].rearrange("t b u -> t (b u)"), in_=hs[:])
            nc.sync.dma_start(out=out_1[0:1, GB * g:GB * (g + 1), :].rearrange("o b u -> o (b u)"), in_=hs[T - 1:T, :])

        def tail_piece(g, b, tcn, o, r, ht):
            sl = slice(b * T, (b + 1) * T)
            nc.scalar.activation(out=tcn[:, sl], in_=tl[("c", g)][:, sl], func=AF.Tanh)
            nc.vector.tensor_tensor(out=r[:, sl], in0=o[:, sl], in1=tcn[:, sl], op=ALU.mult)
            nc.tensor.transpose(ht[:, (b % 2) * H:(b % 2 + 1) * H], r[:, sl], ident_f[:])

        ident_f = const.tile([P, P], F32, name="ident_f", tag="ident_f")
        make_identity(nc, ident_f[:])
        ident_b = const.tile([P, P], BF16, name="ident_b", tag="ident_b")
        make_identity(nc, ident_b[:])
        w_sb = const.tile([P, 4 * I], BF16, name="w_sb", tag="w_sb")
        w_dst = w_sb[:].rearrange("p (j k) -> p j k", j=4)
        w_src = w_ih.rearrange("(j p) k -> p j k", p=P)
        nc.sync.dma_start(out=w_dst[:, 0:2], in_=w_src[:, 0:2])
        nc.sync.dma_start(out=w_dst[:, 2:4], in_=w_src[:, 2:4])
        load(0)
        whh_sb = const.tile([P, 4 * H], BF16, name="whh_sb", tag="whh_sb")
        nc.scalar.dma_start(out=whh_sb[:].rearrange("p (j k) -> p j k", j=4), in_=w_hh.rearrange("(j p) k -> p j k", p=P))
        h0_sb = const.tile([P, H], BF16, name="h0_sb", tag="h0_sb")
        nc.scalar.dma_start(out=h0_sb[:], in_=h0)
        bz = const.tile([P, 4 * H], BF16, name="bz", tag="bz")
        nc.vector.memset(bz[:], 0.0)
        ones = const.tile([P, B], BF16, name="ones", tag="ones")
        nc.vector.memset(ones[:], 1.0)
        nc.scalar.dma_start(out=bz[0:1, :], in_=b_ih.rearrange("(o n) -> o n", o=1))
        nc.scalar.dma_start(out=bz[1:2, :], in_=b_hh.rearrange("(o n) -> o n", o=1))
        c0_sb = const.tile([P, H], BF16, name="c0_sb", tag="c0_sb")
        nc.scalar.dma_start(out=c0_sb[:], in_=c0)
        for g in range(1, 3):
            load(g)
        load_noise(0)
        for g in range(3, LEAD):
            load(g)
        load_noise(1)

        cl = const.tile([P, B], F32, name="cl", tag="cl")

        w_grp, w_gv, w_halves = transposes_in(w_sb[:].bitcast(F32), "w", tag="ht")
        nc.vector.tensor_copy(out=w_gv[:, 0:2], in_=w_halves[0][:].rearrange("p b u r -> p b r u"))
        nc.scalar.copy(out=w_gv[:, 2:4], in_=w_halves[1][:].rearrange("p b u r -> p b r u"))
        w_codes = const.tile([P, 4 * H], U32, name="w_codes", tag="w_codes", align_bytes=64)
        w_scl = const.tile([P, 4 * H], U8, name="w_scl", tag="w_scl", align_bytes=64)
        t_in(0)
        evac_in(0, second_on_act=True)
        nc.vector.quantize_mx(out=w_codes[:].bitcast(FP8X4), scales=w_scl[:], in_=w_grp[:])
        quant(0)

        sm_ps = ps1.tile([P, 6, P], BF16, name="sm_ps", tag="gp3")
        for j in range(4):
            nc.tensor.transpose(sm_ps[:, j, :], whh_sb[:, j * H:(j + 1) * H], ident_b[:])
        nc.tensor.transpose(sm_ps[:, 4, :], h0_sb[:], ident_b[:])
        nc.tensor.transpose(sm_ps[:, 5, :], c0_sb[:], ident_b[:])
        sm_t = const.tile([P, 5, P], BF16, name="sm_t", tag="sm_t")
        nc.scalar.copy(out=sm_t[:], in_=sm_ps[:, 0:5, :])
        c0t = const.tile([P, B], F32, name="c0t", tag="c0t")
        t_in(1)
        g_ps = ps1.tile([P, 4 * B], F32, name="g_ps", tag="gp1")
        for j in range(4):
            nc.tensor.matmul(g_ps[:, j * B:(j + 1) * B], lhsT=sm_t[:, j, :], rhs=sm_t[:, 4, :], start=True, stop=False)
            nc.tensor.matmul(g_ps[:, j * B:(j + 1) * B], lhsT=bz[:, j * H:(j + 1) * H], rhs=ones[:], start=False, stop=True)
        gt = const.tile([P, 4 * B], F32, name="gt", tag="gt")
        nc.scalar.copy(out=gt[:], in_=g_ps[:])
        nc.scalar.copy(out=c0t[:], in_=sm_ps[:, 5, :])
        mx(0)
        evac_in(1, second_on_act=False)
        quant(1)
        t_in(2)
        evac_in(2, second_on_act=False)

        for it in range(NG):
            if it + LEAD < NG:
                load(it + LEAD)
            if it % GPC == 0 and it // GPC + 2 < NCH:
                load_noise(it // GPC + 2)
            if 0 <= it - 1:
                cell(it - 1)
            if it + 3 < NG:
                t_in(it + 3)
            if 0 <= it - 2:
                r_mul(it - 2)
                t_out(it - 2)
            if it + 1 < NG:
                mx(it + 1)
            acts(it, GATE_ORDER[0:2])
            if 0 <= it - 3:
                h_out(it - 3)
            if it + 3 < NG:
                evac_in(it + 3)
            acts(it, GATE_ORDER[2:4])
            if 0 <= it - 1:
                cl_copy(it - 1)
            if it == NG - 1:
                cell(it)
                cl_copy(it)
            if 0 <= it - 1:
                tanh_c(it - 1)
            if it + 2 < NG:
                quant(it + 2)

        r_mul(NG - 2)
        t_out(NG - 2)
        h_out(NG - 3)
        g = NG - 1
        cl_ps = ps2.tile([P, H], F32, name="cl_ps", tag="xt")
        nc.tensor.transpose(cl_ps[:], cl[:], ident_f[:])
        tcn = work.tile([P, COLS], F32, name="tc_last", tag="tc")
        r = work.tile([P, COLS], F32, name="r_last", tag="r")
        o = tl.pop(("gs", 3, g))
        ht_halves = [ps1.tile([P, 2 * H], F32, name="ht_last0", tag="gp0"), ps1.tile([P, 2 * H], F32, name="ht_last1", tag="gp2")]
        hs = work.tile([P, COLS], F32, name="hs_last", tag="hs")
        nz = tl[("nz", g // GPC)]
        k = g % GPC
        for b in range(GB):
            tail_piece(g, b, tcn, o, r, ht_halves[b // 2])
        h_out(NG - 2)
        cl_sb = const.tile([P, H], F32, name="cl_sb", tag="cl_sb")
        nc.vector.tensor_copy(out=cl_sb[:], in_=cl_ps[:])
        nc.sync.dma_start(out=out_1[1], in_=cl_sb[:])
        for hf in range(2):
            sl = slice(hf * 2 * T, (hf + 1) * 2 * T)
            nc.vector.tensor_tensor(out=hs[:, sl], in0=ht_halves[hf][:], in1=nz[:, k * COLS + hf * 2 * T:k * COLS + (hf + 1) * 2 * T], op=ALU.add)
            nc.sync.dma_start(out=out_0[:, GB * g + 2 * hf:GB * g + 2 * hf + 2, :].rearrange("t b u -> t (b u)"), in_=hs[:, sl])
        nc.sync.dma_start(out=out_1[0:1, GB * g:GB * (g + 1), :].rearrange("o b u -> o (b u)"), in_=hs[T - 1:T, :])
